import numpy as np
import ml_dtypes


def mxq(x, axis, fmt="e4m3"):
    dtype, down = {"e4m3": (ml_dtypes.float8_e4m3fn, 7), "e5m2": (ml_dtypes.float8_e5m2, 14)}[fmt]
    v = np.moveaxis(np.asarray(x, np.float32).astype(ml_dtypes.bfloat16).astype(np.float64), axis, -1)
    blocks = v.reshape(v.shape[:-1] + (-1, 32))
    amax = np.abs(blocks).max(-1, keepdims=True)
    byte = np.maximum(np.where(amax > 0, np.frexp(amax)[1] - 1 + 127, 0) - down, 1)
    scale = np.exp2(byte - 127.0)
    codes = (blocks / scale).astype(np.float32).astype(dtype).astype(np.float64)
    return np.moveaxis((codes * scale).reshape(v.shape), -1, axis)


WIDE = False


def mx_kscale(k):
    if not WIDE:
        return np.ones(k)
    levels = np.array([10, -10, 5, -5, 0])
    a = np.random.permutation(np.resize(levels, k // 512 * 4)).reshape(k // 512, 4)
    idx = np.arange(k)
    return np.exp2(a[idx // 512, idx % 128 // 32])


BF16 = ml_dtypes.bfloat16


def bf(x):
    return np.asarray(x, np.float32).astype(BF16)


def f64(x):
    return np.asarray(x).astype(np.float64)


B, L, C, K, D_MODEL, H, D_LLM = 2, 32, 16, 100, 512, 32, 128
D_KEYS = D_MODEL // H
G = H * D_KEYS


def setup_inputs():
    s = mx_kscale(G).reshape(H, D_KEYS)
    return {
        "attn_ctx": bf(np.random.standard_normal((B, C, L, H, D_KEYS)) * 0.5 * s),
        "Wo": bf(np.random.standard_normal((C, H, D_KEYS, D_LLM)) * 2.0 / np.sqrt(G) / s[:, :, None]),
        "bo": bf(np.random.standard_normal((C, D_LLM)) * 0.5),
        "cluster_probs": bf(np.random.uniform(size=(B, L, C))),
    }


def reference(attn_ctx, Wo, bo, cluster_probs):
    o = f64(attn_ctx).reshape(B, C, L, G)
    w = f64(Wo).reshape(C, G, D_LLM)
    proj = mxq(o, 3, "e4m3") @ mxq(w, 1, "e4m3")
    aligned = proj.transpose(0, 2, 1, 3) + f64(bo)
    return (aligned * f64(cluster_probs)[:, :, :, None]).sum(-2)

@@ -1,0 +1,159 @@
+import concourse.mybir as mybir
+from concourse.masks import make_identity
+
+BF16 = mybir.dt.bfloat16
+F32 = mybir.dt.float32
+I32 = mybir.dt.int32
+U32 = mybir.dt.uint32
+U8 = mybir.dt.uint8
+FP8X4 = mybir.dt.float8_e4m3fn_x4
+MULT = mybir.AluOpType.mult
+ADD = mybir.AluOpType.add
+
+P = 128
+PACK = 4
+B, C, L, G, E = 2, 16, 32, 512, 128
+TOKENS = B * L
+PAIRS = C // 2
+ROW_TILES = L * C // P
+CLUSTERS_PER_TILE = P // L
+WORDS = G // 2
+
+FLOPS = 2 * B * C * L * G * E
+
+
+def tile_model_pa_s_kernel(tc, attn_ctx, Wo, bo, cluster_probs, out):
+    nc = tc.nc
+    ctx_rows = attn_ctx.rearrange("b c l h d -> b (c l) (h d)")
+    w_rows = Wo.rearrange("c h d e -> c (h d) e")
+    probs_rows = cluster_probs.rearrange("b l c -> (b l) c")
+
+    with tc.tile_pool(name="keep", bufs=1) as keep, tc.psum_pool(name="psum", bufs=1) as psum:
+        ctx_raw = []
+        for b in range(B):
+            raw = keep.tile([P, ROW_TILES, G], BF16, name="ctx_raw%d" % b)
+            nc.sync.dma_start(out=raw[:], in_=ctx_rows[b].rearrange("(i p) k -> p i k", p=P))
+            ctx_raw.append(raw)
+        w_raw = []
+        for i in range(PAIRS):
+            raw = keep.tile([P, 2, PACK, E], BF16, name="w_raw%d" % i)
+            nc.sync.dma_start(
+                out=raw[:].rearrange("p s j e -> p s (j e)"),
+                in_=w_rows[2 * i : 2 * i + 2].rearrange("s (p j) e -> p s (j e)", j=PACK),
+            )
+            w_raw.append(raw)
+
+        ident_f32 = keep.tile([P, P], F32)
+        make_identity(nc, ident_f32[:])
+        ident_bf16 = keep.tile([P, P], BF16)
+        nc.vector.tensor_copy(out=ident_bf16[:], in_=ident_f32[:])
+        fold = keep.tile([P, 2, TOKENS], F32)
+        for half in range(2):
+            nc.vector.tensor_add(
+                out=fold[:, half, :], in0=ident_f32[:, 0:TOKENS], in1=ident_f32[:, TOKENS:P]
+            )
+
+        probs_square = keep.tile([P, P], BF16)
+        nc.vector.memset(probs_square[:], 0.0)
+        nc.scalar.dma_start(out=probs_square[0:TOKENS, 0:C], in_=probs_rows)
+        bias_square = keep.tile([P, E], BF16)
+        nc.vector.memset(bias_square[:], 0.0)
+        nc.scalar.dma_start(out=bias_square[0:C, :], in_=bo)
+        probs_twice = keep.tile([P, PAIRS, 2], BF16)
+        for half in range(2):
+            nc.scalar.dma_start(
+                out=probs_twice[half * TOKENS : (half + 1) * TOKENS].rearrange("p i s -> p (i s)"),
+                in_=probs_rows,
+            )
+        pair_probs = keep.tile([P, PAIRS], F32)
+        for half in range(2):
+            rows = slice(half * TOKENS, (half + 1) * TOKENS)
+            nc.vector.tensor_copy(out=pair_probs[rows, :], in_=probs_twice[rows, :, half])
+
+        ctx_codes = keep.tile([P, PAIRS, 3 * TOKENS], U32, align_bytes=64)
+        ctx_scales = keep.tile([P, PAIRS, 3 * TOKENS], U8, align_bytes=64)
+        nc.vector.memset(ctx_codes[:].bitcast(I32)[:, :, TOKENS : 2 * TOKENS], 0)
+        nc.vector.memset(ctx_scales[:].bitcast(I32)[:, :, TOKENS // 4 : 2 * TOKENS // 4], 0)
+
+        probs_t_psum = psum.tile([P, P], BF16, tag="small", bufs=2)
+        nc.tensor.transpose(probs_t_psum[:], probs_square[:], ident_bf16[:])
+        probs_t = keep.tile([P, P], BF16)
+        nc.scalar.copy(out=probs_t[:], in_=probs_t_psum[:])
+
+        ctx_grouped = keep.tile([P, C, TOKENS, PACK], BF16, align_bytes=64)
+        ctx_grouped_words = ctx_grouped[:].bitcast(F32)
+        for b in range(B):
+            words = ctx_raw[b][:].bitcast(F32).rearrange("p i (q u) -> p i u q", u=2)
+            for h in range(ROW_TILES // 2):
+                ctx_t = psum.tile([P, 2, 2, P], F32, tag="ctx_t", bufs=4)
+                for r in range(2):
+                    for u in range(2):
+                        nc.tensor.transpose(ctx_t[:, u, r, :], words[:, 2 * h + r, u, :], ident_f32[:])
+                first = 2 * h * CLUSTERS_PER_TILE
+                nc.scalar.copy(
+                    out=ctx_grouped_words[
+                        :, first : first + 2 * CLUSTERS_PER_TILE, b * L : (b + 1) * L, :
+                    ],
+                    in_=ctx_t[:].rearrange("q u r (c l) -> q (r c) l u", l=L),
+                )
+
+        bias_psum = psum.tile([P, E], F32, tag="small", bufs=2)
+        nc.tensor.matmul(out=bias_psum[:], lhsT=probs_t[:], rhs=bias_square[:], start=True, stop=True)
+        mixed = keep.tile([P, E], F32)
+        nc.scalar.copy(out=mixed[:], in_=bias_psum[:])
+
+        for c in range(C):
+            i, s = divmod(c, 2)
+            cols = slice(2 * s * TOKENS, (2 * s + 1) * TOKENS)
+            nc.vector.quantize_mx(
+                out=ctx_codes[:, i, cols].bitcast(FP8X4),
+                scales=ctx_scales[:, i, cols],
+                in_=ctx_grouped[:, c, :, :].rearrange("p t j -> p (t j)"),
+            )
+
+        w_codes = keep.tile([P, PAIRS, 2 * E], U32, align_bytes=64)
+        w_scales = keep.tile([P, PAIRS, 2 * E], U8, align_bytes=64)
+        for i in range(PAIRS):
+            w_grouped = keep.tile([P, 2, E, PACK], BF16, name="w_grouped%d" % i, align_bytes=64)
+            nc.vector.tensor_copy(
+                out=w_grouped[:, 0, :, :].rearrange("p (g r) j -> p g j r", r=4),
+                in_=w_raw[i][:, 0, :, :].rearrange("p j (g r) -> p g j r", r=4),
+            )
+            nc.scalar.copy(
+                out=w_grouped[:, 1, :, :].rearrange("p (g r) j -> p g j r", r=4),
+                in_=w_raw[i][:, 1, :, :].rearrange("p j (g r) -> p g j r", r=4),
+            )
+            nc.vector.quantize_mx(
+                out=w_codes[:, i, :].bitcast(FP8X4),
+                scales=w_scales[:, i, :],
+                in_=w_grouped[:].rearrange("p s e j -> p (s e j)"),
+            )
+            product = psum.tile([P, E], F32, tag="product", bufs=2)
+            for s in range(2):
+                tokens = slice(s * TOKENS, s * TOKENS + P)
+                columns = slice(s * E, (s + 1) * E)
+                nc.tensor.matmul_mx(
+                    out=product[:],
+                    lhsT=ctx_codes[:, i, tokens].bitcast(FP8X4),
+                    lhsT_scale=ctx_scales[:, i, tokens],
+                    rhs=w_codes[:, i, columns].bitcast(FP8X4),
+                    rhs_scale=w_scales[:, i, columns],
+                    start=(s == 0),
+                    stop=(s == 1),
+                )
+            nc.vector.scalar_tensor_tensor(
+                out=mixed[:],
+                in0=product[:],
+                scalar=pair_probs[:, i : i + 1],
+                in1=mixed[:],
+                op0=MULT,
+                op1=ADD,
+            )
+
+        fused_psum = psum.tile([P, E], F32, tag="small", bufs=2)
+        nc.tensor.matmul(
+            out=fused_psum[:], lhsT=fold[:].rearrange("p a m -> p (a m)"), rhs=mixed[:], start=True, stop=True
+        )
+        fused = keep.tile([TOKENS, E], F32)
+        nc.vector.tensor_copy(out=fused[:], in_=fused_psum[0:TOKENS, :])
+        nc.sync.dma_start(out=out.rearrange("b l e -> (b l) e"), in_=fused[:])

@@ -15,9 +15,12 @@ PACK = 4
 B, C, L, G, E = 2, 16, 32, 512, 128
 TOKENS = B * L
 PAIRS = C // 2
-ROW_TILES = L * C // P
-CLUSTERS_PER_TILE = P // L
-WORDS = G // 2
+HALVES = 2
+HALF_CLUSTERS = C // HALVES
+ROW_TILES = HALF_CLUSTERS * L // P
+VECTOR_COLUMNS = 96
+MIX_LAG = 3
+PSUM_BANKS = 6
 
 FLOPS = 2 * B * C * L * G * E
 
@@ -28,12 +31,18 @@ def tile_model_pa_s_kernel(tc, attn_ctx, Wo, bo, cluster_probs, out):
     w_rows = Wo.rearrange("c h d e -> c (h d) e")
     probs_rows = cluster_probs.rearrange("b l c -> (b l) c")
 
-    with tc.tile_pool(name="keep", bufs=1) as keep, tc.psum_pool(name="psum", bufs=1) as psum:
-        ctx_raw = []
-        for b in range(B):
-            raw = keep.tile([P, ROW_TILES, G], BF16, name="ctx_raw%d" % b)
-            nc.sync.dma_start(out=raw[:], in_=ctx_rows[b].rearrange("(i p) k -> p i k", p=P))
-            ctx_raw.append(raw)
+    with (
+        tc.tile_pool(name="keep", bufs=1) as keep,
+        tc.psum_pool(name="psum", bufs=1) as psum,
+        tc.manual_schedule(),
+    ):
+        ctx_raw = {}
+        for h in range(HALVES):
+            for b in range(B):
+                raw = keep.tile([P, ROW_TILES, G], BF16, name="ctx_raw%d%d" % (h, b))
+                rows = ctx_rows[b, h * ROW_TILES * P : (h + 1) * ROW_TILES * P, :]
+                nc.sync.dma_start(out=raw[:], in_=rows.rearrange("(r p) k -> p r k", p=P))
+                ctx_raw[(h, b)] = raw
         w_raw = []
         for i in range(PAIRS):
             raw = keep.tile([P, 2, PACK, E], BF16, name="w_raw%d" % i)
@@ -43,97 +52,99 @@ def tile_model_pa_s_kernel(tc, attn_ctx, Wo, bo, cluster_probs, out):
             )
             w_raw.append(raw)
 
-        ident_f32 = keep.tile([P, P], F32)
-        make_identity(nc, ident_f32[:])
-        ident_bf16 = keep.tile([P, P], BF16)
-        nc.vector.tensor_copy(out=ident_bf16[:], in_=ident_f32[:])
-        fold = keep.tile([P, 2, TOKENS], F32)
-        for half in range(2):
-            nc.vector.tensor_add(
-                out=fold[:, half, :], in0=ident_f32[:, 0:TOKENS], in1=ident_f32[:, TOKENS:P]
+        probs_twice = keep.tile([P, PAIRS, 2], BF16)
+        for s in range(2):
+            nc.scalar.dma_start(
+                out=probs_twice[s * TOKENS : (s + 1) * TOKENS].rearrange("p i s -> p (i s)"),
+                in_=probs_rows,
             )
-
         probs_square = keep.tile([P, P], BF16)
         nc.vector.memset(probs_square[:], 0.0)
         nc.scalar.dma_start(out=probs_square[0:TOKENS, 0:C], in_=probs_rows)
         bias_square = keep.tile([P, E], BF16)
         nc.vector.memset(bias_square[:], 0.0)
         nc.scalar.dma_start(out=bias_square[0:C, :], in_=bo)
-        probs_twice = keep.tile([P, PAIRS, 2], BF16)
-        for half in range(2):
-            nc.scalar.dma_start(
-                out=probs_twice[half * TOKENS : (half + 1) * TOKENS].rearrange("p i s -> p (i s)"),
-                in_=probs_rows,
-            )
-        pair_probs = keep.tile([P, PAIRS], F32)
-        for half in range(2):
-            rows = slice(half * TOKENS, (half + 1) * TOKENS)
-            nc.vector.tensor_copy(out=pair_probs[rows, :], in_=probs_twice[rows, :, half])
 
+        ident_f32 = keep.tile([P, P], F32)
+        make_identity(nc, ident_f32[:])
         ctx_codes = keep.tile([P, PAIRS, 3 * TOKENS], U32, align_bytes=64)
         ctx_scales = keep.tile([P, PAIRS, 3 * TOKENS], U8, align_bytes=64)
         nc.vector.memset(ctx_codes[:].bitcast(I32)[:, :, TOKENS : 2 * TOKENS], 0)
         nc.vector.memset(ctx_scales[:].bitcast(I32)[:, :, TOKENS // 4 : 2 * TOKENS // 4], 0)
-
-        probs_t_psum = psum.tile([P, P], BF16, tag="small", bufs=2)
-        nc.tensor.transpose(probs_t_psum[:], probs_square[:], ident_bf16[:])
-        probs_t = keep.tile([P, P], BF16)
-        nc.scalar.copy(out=probs_t[:], in_=probs_t_psum[:])
+        mixed = keep.tile([P, E], F32)
+        nc.vector.memset(mixed[:], 0.0)
+        ident_bf16 = keep.tile([P, P], BF16)
+        nc.vector.tensor_copy(out=ident_bf16[:], in_=ident_f32[:])
+        fold = keep.tile([P, 2, TOKENS], F32)
+        for s in range(2):
+            nc.vector.tensor_add(
+                out=fold[:, s, :], in0=ident_f32[:, 0:TOKENS], in1=ident_f32[:, TOKENS:P]
+            )
 
         ctx_grouped = keep.tile([P, C, TOKENS, PACK], BF16, align_bytes=64)
         ctx_grouped_words = ctx_grouped[:].bitcast(F32)
-        for b in range(B):
-            words = ctx_raw[b][:].bitcast(F32).rearrange("p i (q u) -> p i u q", u=2)
-            for h in range(ROW_TILES // 2):
-                ctx_t = psum.tile([P, 2, 2, P], F32, tag="ctx_t", bufs=4)
-                for r in range(2):
+        for h in range(HALVES):
+            clusters = slice(h * HALF_CLUSTERS, (h + 1) * HALF_CLUSTERS)
+            for b in range(B):
+                words = ctx_raw[(h, b)][:].bitcast(F32).rearrange("p r (q u) -> p r u q", u=2)
+                ctx_t = psum.tile([P, 2, ROW_TILES, P], F32, tag="bank", bufs=PSUM_BANKS)
+                for r in range(ROW_TILES):
                     for u in range(2):
-                        nc.tensor.transpose(ctx_t[:, u, r, :], words[:, 2 * h + r, u, :], ident_f32[:])
-                first = 2 * h * CLUSTERS_PER_TILE
+                        nc.tensor.transpose(ctx_t[:, u, r, :], words[:, r, u, :], ident_f32[:])
                 nc.scalar.copy(
-                    out=ctx_grouped_words[
-                        :, first : first + 2 * CLUSTERS_PER_TILE, b * L : (b + 1) * L, :
-                    ],
+                    out=ctx_grouped_words[:, clusters, b * L : (b + 1) * L, :],
                     in_=ctx_t[:].rearrange("q u r (c l) -> q (r c) l u", l=L),
                 )
+            for c in range(h * HALF_CLUSTERS, (h + 1) * HALF_CLUSTERS):
+                i, s = divmod(c, 2)
+                columns = slice(2 * s * TOKENS, (2 * s + 1) * TOKENS)
+                nc.vector.quantize_mx(
+                    out=ctx_codes[:, i, columns].bitcast(FP8X4),
+                    scales=ctx_scales[:, i, columns],
+                    in_=ctx_grouped[:, c, :, :].rearrange("p t j -> p (t j)"),
+                )
 
-        bias_psum = psum.tile([P, E], F32, tag="small", bufs=2)
-        nc.tensor.matmul(out=bias_psum[:], lhsT=probs_t[:], rhs=bias_square[:], start=True, stop=True)
-        mixed = keep.tile([P, E], F32)
-        nc.scalar.copy(out=mixed[:], in_=bias_psum[:])
-
-        for c in range(C):
-            i, s = divmod(c, 2)
-            cols = slice(2 * s * TOKENS, (2 * s + 1) * TOKENS)
-            nc.vector.quantize_mx(
-                out=ctx_codes[:, i, cols].bitcast(FP8X4),
-                scales=ctx_scales[:, i, cols],
-                in_=ctx_grouped[:, c, :, :].rearrange("p t j -> p (t j)"),
-            )
+        probs_t_psum = psum.tile([P, P], BF16, tag="probs_t")
+        nc.tensor.transpose(probs_t_psum[:], probs_square[:], ident_bf16[:])
+        probs_t = keep.tile([P, P], BF16)
+        nc.scalar.copy(out=probs_t[:], in_=probs_t_psum[:])
+        fused_psum = psum.tile([P, E], F32, tag="fused")
+        nc.tensor.matmul(out=fused_psum[:], lhsT=probs_t[:], rhs=bias_square[:], start=True, stop=False)
+        pair_probs = keep.tile([P, PAIRS], F32)
+        for s in range(2):
+            rows = slice(s * TOKENS, (s + 1) * TOKENS)
+            nc.vector.tensor_copy(out=pair_probs[rows, :], in_=probs_twice[rows, :, s])
 
         w_codes = keep.tile([P, PAIRS, 2 * E], U32, align_bytes=64)
         w_scales = keep.tile([P, PAIRS, 2 * E], U8, align_bytes=64)
-        for i in range(PAIRS):
-            w_grouped = keep.tile([P, 2, E, PACK], BF16, name="w_grouped%d" % i, align_bytes=64)
-            nc.vector.tensor_copy(
-                out=w_grouped[:, 0, :, :].rearrange("p (g r) j -> p g j r", r=4),
-                in_=w_raw[i][:, 0, :, :].rearrange("p j (g r) -> p g j r", r=4),
+        w_grouped = [
+            keep.tile([P, 2, E, PACK], BF16, name="w_grouped%d" % i, align_bytes=64) for i in range(PAIRS)
+        ]
+        products = {}
+
+        def regroup(copy, i, s, columns):
+            copy(
+                out=w_grouped[i][:, s, columns, :].rearrange("p (g r) j -> p g j r", r=4),
+                in_=w_raw[i][:, s, :, columns].rearrange("p j (g r) -> p g j r", r=4),
             )
-            nc.scalar.copy(
-                out=w_grouped[:, 1, :, :].rearrange("p (g r) j -> p g j r", r=4),
-                in_=w_raw[i][:, 1, :, :].rearrange("p j (g r) -> p g j r", r=4),
-            )
+
+        def regroup_pair(i):
+            regroup(nc.vector.tensor_copy, i, 0, slice(0, VECTOR_COLUMNS))
+            regroup(nc.scalar.copy, i, 0, slice(VECTOR_COLUMNS, E))
+            regroup(nc.scalar.copy, i, 1, slice(0, E))
+
+        def quantise_and_multiply(i):
             nc.vector.quantize_mx(
                 out=w_codes[:, i, :].bitcast(FP8X4),
                 scales=w_scales[:, i, :],
-                in_=w_grouped[:].rearrange("p s e j -> p (s e j)"),
+                in_=w_grouped[i][:].rearrange("p s e j -> p (s e j)"),
             )
-            product = psum.tile([P, E], F32, tag="product", bufs=2)
+            products[i] = psum.tile([P, E], F32, name="product%d" % i, tag="bank", bufs=PSUM_BANKS)
             for s in range(2):
                 tokens = slice(s * TOKENS, s * TOKENS + P)
                 columns = slice(s * E, (s + 1) * E)
                 nc.tensor.matmul_mx(
-                    out=product[:],
+                    out=products[i][:],
                     lhsT=ctx_codes[:, i, tokens].bitcast(FP8X4),
                     lhsT_scale=ctx_scales[:, i, tokens],
                     rhs=w_codes[:, i, columns].bitcast(FP8X4),
@@ -141,18 +152,27 @@ def tile_model_pa_s_kernel(tc, attn_ctx, Wo, bo, cluster_probs, out):
                     start=(s == 0),
                     stop=(s == 1),
                 )
+
+        def mix(i):
             nc.vector.scalar_tensor_tensor(
                 out=mixed[:],
-                in0=product[:],
+                in0=products[i][:],
                 scalar=pair_probs[:, i : i + 1],
                 in1=mixed[:],
                 op0=MULT,
                 op1=ADD,
             )
 
-        fused_psum = psum.tile([P, E], F32, tag="small", bufs=2)
+        for step in range(PAIRS + MIX_LAG):
+            if step < PAIRS:
+                regroup_pair(step)
+            if 1 <= step <= PAIRS:
+                quantise_and_multiply(step - 1)
+            if step >= MIX_LAG:
+                mix(step - MIX_LAG)
+
         nc.tensor.matmul(
-            out=fused_psum[:], lhsT=fold[:].rearrange("p a m -> p (a m)"), rhs=mixed[:], start=True, stop=True
+            out=fused_psum[:], lhsT=fold[:].rearrange("p a m -> p (a m)"), rhs=mixed[:], start=False, stop=True
         )
         fused = keep.tile([TOKENS, E], F32)
         nc.vector.tensor_copy(out=fused[:], in_=fused_psum[0:TOKENS, :])

@@ -15,9 +15,8 @@ PACK = 4
 B, C, L, G, E = 2, 16, 32, 512, 128
 TOKENS = B * L
 PAIRS = C // 2
-HALVES = 2
-HALF_CLUSTERS = C // HALVES
-ROW_TILES = HALF_CLUSTERS * L // P
+GROUP = P // L
+GROUPS = C // GROUP
 VECTOR_COLUMNS = 96
 MIX_LAG = 3
 PSUM_BANKS = 6
@@ -27,7 +26,7 @@ FLOPS = 2 * B * C * L * G * E
 
 def tile_model_pa_s_kernel(tc, attn_ctx, Wo, bo, cluster_probs, out):
     nc = tc.nc
-    ctx_rows = attn_ctx.rearrange("b c l h d -> b (c l) (h d)")
+    ctx_rows = attn_ctx.rearrange("b (g c) l h d -> g (c l) b (h d)", c=GROUP)
     w_rows = Wo.rearrange("c h d e -> c (h d) e")
     probs_rows = cluster_probs.rearrange("b l c -> (b l) c")
 
@@ -36,13 +35,11 @@ def tile_model_pa_s_kernel(tc, attn_ctx, Wo, bo, cluster_probs, out):
         tc.psum_pool(name="psum", bufs=1) as psum,
         tc.manual_schedule(),
     ):
-        ctx_raw = {}
-        for h in range(HALVES):
-            for b in range(B):
-                raw = keep.tile([P, ROW_TILES, G], BF16, name="ctx_raw%d%d" % (h, b))
-                rows = ctx_rows[b, h * ROW_TILES * P : (h + 1) * ROW_TILES * P, :]
-                nc.sync.dma_start(out=raw[:], in_=rows.rearrange("(r p) k -> p r k", p=P))
-                ctx_raw[(h, b)] = raw
+        ctx_raw = []
+        for g in range(GROUPS):
+            raw = keep.tile([P, B, G], BF16, name="ctx_raw%d" % g)
+            nc.sync.dma_start(out=raw[:], in_=ctx_rows[g])
+            ctx_raw.append(raw)
         w_raw = []
         for i in range(PAIRS):
             raw = keep.tile([P, 2, PACK, E], BF16, name="w_raw%d" % i)
@@ -83,19 +80,19 @@ def tile_model_pa_s_kernel(tc, attn_ctx, Wo, bo, cluster_probs, out):
 
         ctx_grouped = keep.tile([P, C, TOKENS, PACK], BF16, align_bytes=64)
         ctx_grouped_words = ctx_grouped[:].bitcast(F32)
-        for h in range(HALVES):
-            clusters = slice(h * HALF_CLUSTERS, (h + 1) * HALF_CLUSTERS)
+        for g in range(GROUPS):
+            clusters = slice(g * GROUP, (g + 1) * GROUP)
+            words = ctx_raw[g][:].bitcast(F32).rearrange("p b (q u) -> p b u q", u=2)
             for b in range(B):
-                words = ctx_raw[(h, b)][:].bitcast(F32).rearrange("p r (q u) -> p r u q", u=2)
-                ctx_t = psum.tile([P, 2, ROW_TILES, P], F32, tag="bank", bufs=PSUM_BANKS)
-                for r in range(ROW_TILES):
-                    for u in range(2):
-                        nc.tensor.transpose(ctx_t[:, u, r, :], words[:, r, u, :], ident_f32[:])
-                nc.scalar.copy(
+                ctx_t = psum.tile([P, 2, P], F32, tag="bank", bufs=PSUM_BANKS)
+                for u in range(2):
+                    nc.tensor.transpose(ctx_t[:, u, :], words[:, b, u, :], ident_f32[:])
+                copy_out = nc.scalar.copy if b == 0 else nc.vector.tensor_copy
+                copy_out(
                     out=ctx_grouped_words[:, clusters, b * L : (b + 1) * L, :],
-                    in_=ctx_t[:].rearrange("q u r (c l) -> q (r c) l u", l=L),
+                    in_=ctx_t[:].rearrange("q u (c l) -> q c l u", l=L),
                 )
-            for c in range(h * HALF_CLUSTERS, (h + 1) * HALF_CLUSTERS):
+            for c in range(g * GROUP, (g + 1) * GROUP):
                 i, s = divmod(c, 2)
                 columns = slice(2 * s * TOKENS, (2 * s + 1) * TOKENS)
                 nc.vector.quantize_mx(

@@ -17,7 +17,6 @@ TOKENS = B * L
 PAIRS = C // 2
 GROUP = P // L
 GROUPS = C // GROUP
-VECTOR_COLUMNS = 96
 MIX_LAG = 3
 PSUM_BANKS = 6
 
@@ -36,18 +35,18 @@ def tile_model_pa_s_kernel(tc, attn_ctx, Wo, bo, cluster_probs, out):
         tc.manual_schedule(),
     ):
         ctx_raw = []
+        w_raw = []
         for g in range(GROUPS):
             raw = keep.tile([P, B, G], BF16, name="ctx_raw%d" % g)
             nc.sync.dma_start(out=raw[:], in_=ctx_rows[g])
             ctx_raw.append(raw)
-        w_raw = []
-        for i in range(PAIRS):
-            raw = keep.tile([P, 2, PACK, E], BF16, name="w_raw%d" % i)
-            nc.sync.dma_start(
-                out=raw[:].rearrange("p s j e -> p s (j e)"),
-                in_=w_rows[2 * i : 2 * i + 2].rearrange("s (p j) e -> p s (j e)", j=PACK),
-            )
-            w_raw.append(raw)
+            for i in (2 * g, 2 * g + 1):
+                raw = keep.tile([P, 2, PACK, E], BF16, name="w_raw%d" % i)
+                nc.sync.dma_start(
+                    out=raw[:].rearrange("p s j e -> p s (j e)"),
+                    in_=w_rows[2 * i : 2 * i + 2].rearrange("s (p j) e -> p s (j e)", j=PACK),
+                )
+                w_raw.append(raw)
 
         probs_twice = keep.tile([P, PAIRS, 2], BF16)
         for s in range(2):
@@ -80,18 +79,38 @@ def tile_model_pa_s_kernel(tc, attn_ctx, Wo, bo, cluster_probs, out):
 
         ctx_grouped = keep.tile([P, C, TOKENS, PACK], BF16, align_bytes=64)
         ctx_grouped_words = ctx_grouped[:].bitcast(F32)
-        for g in range(GROUPS):
-            clusters = slice(g * GROUP, (g + 1) * GROUP)
+        ctx_t = {}
+        w_codes = keep.tile([P, PAIRS, 2 * E], U32, align_bytes=64)
+        w_scales = keep.tile([P, PAIRS, 2 * E], U8, align_bytes=64)
+        w_grouped = [
+            keep.tile([P, 2, E, PACK], BF16, name="w_grouped%d" % i, align_bytes=64) for i in range(PAIRS)
+        ]
+        products = {}
+        pair_probs = keep.tile([P, PAIRS], F32)
+
+        def transpose_group(g):
+            if g >= GROUPS:
+                return
             words = ctx_raw[g][:].bitcast(F32).rearrange("p b (q u) -> p b u q", u=2)
             for b in range(B):
-                ctx_t = psum.tile([P, 2, P], F32, tag="bank", bufs=PSUM_BANKS)
-                for u in range(2):
-                    nc.tensor.transpose(ctx_t[:, u, :], words[:, b, u, :], ident_f32[:])
-                copy_out = nc.scalar.copy if b == 0 else nc.vector.tensor_copy
-                copy_out(
-                    out=ctx_grouped_words[:, clusters, b * L : (b + 1) * L, :],
-                    in_=ctx_t[:].rearrange("q u (c l) -> q c l u", l=L),
+                ctx_t[(g, b)] = psum.tile(
+                    [P, 2, P], F32, name="ctx_t%d%d" % (g, b), tag="bank", bufs=PSUM_BANKS
                 )
+                for u in range(2):
+                    nc.tensor.transpose(ctx_t[(g, b)][:, u, :], words[:, b, u, :], ident_f32[:])
+
+        def copy_group(g):
+            if g >= GROUPS:
+                return
+            for b in range(B):
+                nc.scalar.copy(
+                    out=ctx_grouped_words[:, g * GROUP : (g + 1) * GROUP, b * L : (b + 1) * L, :],
+                    in_=ctx_t[(g, b)][:].rearrange("q u (c l) -> q c l u", l=L),
+                )
+
+        def quantise_group(g):
+            if g >= GROUPS:
+                return
             for c in range(g * GROUP, (g + 1) * GROUP):
                 i, s = divmod(c, 2)
                 columns = slice(2 * s * TOKENS, (2 * s + 1) * TOKENS)
@@ -101,41 +120,27 @@ def tile_model_pa_s_kernel(tc, attn_ctx, Wo, bo, cluster_probs, out):
                     in_=ctx_grouped[:, c, :, :].rearrange("p t j -> p (t j)"),
                 )
 
-        probs_t_psum = psum.tile([P, P], BF16, tag="probs_t")
-        nc.tensor.transpose(probs_t_psum[:], probs_square[:], ident_bf16[:])
-        probs_t = keep.tile([P, P], BF16)
-        nc.scalar.copy(out=probs_t[:], in_=probs_t_psum[:])
-        fused_psum = psum.tile([P, E], F32, tag="fused")
-        nc.tensor.matmul(out=fused_psum[:], lhsT=probs_t[:], rhs=bias_square[:], start=True, stop=False)
-        pair_probs = keep.tile([P, PAIRS], F32)
-        for s in range(2):
-            rows = slice(s * TOKENS, (s + 1) * TOKENS)
-            nc.vector.tensor_copy(out=pair_probs[rows, :], in_=probs_twice[rows, :, s])
-
-        w_codes = keep.tile([P, PAIRS, 2 * E], U32, align_bytes=64)
-        w_scales = keep.tile([P, PAIRS, 2 * E], U8, align_bytes=64)
-        w_grouped = [
-            keep.tile([P, 2, E, PACK], BF16, name="w_grouped%d" % i, align_bytes=64) for i in range(PAIRS)
-        ]
-        products = {}
-
-        def regroup(copy, i, s, columns):
-            copy(
-                out=w_grouped[i][:, s, columns, :].rearrange("p (g r) j -> p g j r", r=4),
-                in_=w_raw[i][:, s, :, columns].rearrange("p j (g r) -> p g j r", r=4),
-            )
-
         def regroup_pair(i):
-            regroup(nc.vector.tensor_copy, i, 0, slice(0, VECTOR_COLUMNS))
-            regroup(nc.scalar.copy, i, 0, slice(VECTOR_COLUMNS, E))
-            regroup(nc.scalar.copy, i, 1, slice(0, E))
+            if i >= PAIRS:
+                return
+            for s, copy in ((0, nc.vector.tensor_copy), (1, nc.scalar.copy)):
+                copy(
+                    out=w_grouped[i][:, s, :, :].rearrange("p (g r) j -> p g j r", r=4),
+                    in_=w_raw[i][:, s, :, :].rearrange("p j (g r) -> p g j r", r=4),
+                )
 
-        def quantise_and_multiply(i):
+        def quantise_pair(i):
+            if not 0 <= i < PAIRS:
+                return
             nc.vector.quantize_mx(
                 out=w_codes[:, i, :].bitcast(FP8X4),
                 scales=w_scales[:, i, :],
                 in_=w_grouped[i][:].rearrange("p s e j -> p (s e j)"),
             )
+
+        def multiply_pair(i):
+            if not 0 <= i < PAIRS:
+                return
             products[i] = psum.tile([P, E], F32, name="product%d" % i, tag="bank", bufs=PSUM_BANKS)
             for s in range(2):
                 tokens = slice(s * TOKENS, s * TOKENS + P)
@@ -150,7 +155,9 @@ def tile_model_pa_s_kernel(tc, attn_ctx, Wo, bo, cluster_probs, out):
                     stop=(s == 1),
                 )
 
-        def mix(i):
+        def mix_pair(i):
+            if not 0 <= i < PAIRS:
+                return
             nc.vector.scalar_tensor_tensor(
                 out=mixed[:],
                 in0=products[i][:],
@@ -160,13 +167,32 @@ def tile_model_pa_s_kernel(tc, attn_ctx, Wo, bo, cluster_probs, out):
                 op1=ADD,
             )
 
-        for step in range(PAIRS + MIX_LAG):
-            if step < PAIRS:
-                regroup_pair(step)
-            if 1 <= step <= PAIRS:
-                quantise_and_multiply(step - 1)
-            if step >= MIX_LAG:
-                mix(step - MIX_LAG)
+        transpose_group(0)
+        copy_group(0)
+
+        probs_t_psum = psum.tile([P, P], BF16, tag="probs_t")
+        nc.tensor.transpose(probs_t_psum[:], probs_square[:], ident_bf16[:])
+        probs_t = keep.tile([P, P], BF16)
+        nc.scalar.copy(out=probs_t[:], in_=probs_t_psum[:])
+        fused_psum = psum.tile([P, E], F32, tag="fused")
+        nc.tensor.matmul(out=fused_psum[:], lhsT=probs_t[:], rhs=bias_square[:], start=True, stop=False)
+        for s in range(2):
+            rows = slice(s * TOKENS, (s + 1) * TOKENS)
+            nc.vector.tensor_copy(out=pair_probs[rows, :], in_=probs_twice[rows, :, s])
+
+        for g in range(GROUPS + 2):
+            first, second = 2 * g, 2 * g + 1
+            transpose_group(g + 1)
+            regroup_pair(first)
+            quantise_pair(first - 1)
+            quantise_group(g)
+            multiply_pair(first - 1)
+            mix_pair(first - MIX_LAG)
+            regroup_pair(second)
+            copy_group(g + 1)
+            quantise_pair(second - 1)
+            multiply_pair(second - 1)
+            mix_pair(second - MIX_LAG)
 
         nc.tensor.matmul(
             out=fused_psum[:], lhsT=fold[:].rearrange("p a m -> p (a m)"), rhs=mixed[:], start=False, stop=True

@@ -15,6 +15,8 @@ PACK = 4
 B, C, L, G, E = 2, 16, 32, 512, 128
 TOKENS = B * L
 PAIRS = C // 2
+FOLDED_PAIRS = PAIRS - 1
+BLOCKS = 3 * PAIRS + 1
 GROUP = P // L
 GROUPS = C // GROUP
 MIX_LAG = 3
@@ -48,12 +50,9 @@ def tile_model_pa_s_kernel(tc, attn_ctx, Wo, bo, cluster_probs, out):
                 )
                 w_raw.append(raw)
 
-        probs_twice = keep.tile([P, PAIRS, 2], BF16)
+        probs_twice = keep.tile([P, C], BF16)
         for s in range(2):
-            nc.scalar.dma_start(
-                out=probs_twice[s * TOKENS : (s + 1) * TOKENS].rearrange("p i s -> p (i s)"),
-                in_=probs_rows,
-            )
+            nc.scalar.dma_start(out=probs_twice[s * TOKENS : (s + 1) * TOKENS, :], in_=probs_rows)
         probs_square = keep.tile([P, P], BF16)
         nc.vector.memset(probs_square[:], 0.0)
         nc.scalar.dma_start(out=probs_square[0:TOKENS, 0:C], in_=probs_rows)
@@ -63,12 +62,14 @@ def tile_model_pa_s_kernel(tc, attn_ctx, Wo, bo, cluster_probs, out):
 
         ident_f32 = keep.tile([P, P], F32)
         make_identity(nc, ident_f32[:])
-        ctx_codes = keep.tile([P, PAIRS, 3 * TOKENS], U32, align_bytes=64)
-        ctx_scales = keep.tile([P, PAIRS, 3 * TOKENS], U8, align_bytes=64)
-        nc.vector.memset(ctx_codes[:].bitcast(I32)[:, :, TOKENS : 2 * TOKENS], 0)
-        nc.vector.memset(ctx_scales[:].bitcast(I32)[:, :, TOKENS // 4 : 2 * TOKENS // 4], 0)
+        ctx_codes = keep.tile([P, BLOCKS, TOKENS], U32, align_bytes=64)
+        ctx_scales = keep.tile([P, BLOCKS, TOKENS], U8, align_bytes=64)
+        nc.vector.memset(ctx_codes[:].bitcast(I32), 0)
+        nc.vector.memset(ctx_scales[:].bitcast(I32), 0)
         mixed = keep.tile([P, E], F32)
         nc.vector.memset(mixed[:], 0.0)
+        late = keep.tile([TOKENS, E], F32)
+        nc.vector.memset(late[:], 0.0)
         ident_bf16 = keep.tile([P, P], BF16)
         nc.vector.tensor_copy(out=ident_bf16[:], in_=ident_f32[:])
         fold = keep.tile([P, 2, TOKENS], F32)
@@ -86,7 +87,7 @@ def tile_model_pa_s_kernel(tc, attn_ctx, Wo, bo, cluster_probs, out):
             keep.tile([P, 2, E, PACK], BF16, name="w_grouped%d" % i, align_bytes=64) for i in range(PAIRS)
         ]
         products = {}
-        pair_probs = keep.tile([P, PAIRS], F32)
+        weights = keep.tile([P, C], F32)
 
         def transpose_group(g):
             if g >= GROUPS:
@@ -113,10 +114,9 @@ def tile_model_pa_s_kernel(tc, attn_ctx, Wo, bo, cluster_probs, out):
                 return
             for c in range(g * GROUP, (g + 1) * GROUP):
                 i, s = divmod(c, 2)
-                columns = slice(2 * s * TOKENS, (2 * s + 1) * TOKENS)
                 nc.vector.quantize_mx(
-                    out=ctx_codes[:, i, columns].bitcast(FP8X4),
-                    scales=ctx_scales[:, i, columns],
+                    out=ctx_codes[:, 3 * i + 2 * s, :].bitcast(FP8X4),
+                    scales=ctx_scales[:, 3 * i + 2 * s, :],
                     in_=ctx_grouped[:, c, :, :].rearrange("p t j -> p (t j)"),
                 )
 
@@ -138,34 +138,60 @@ def tile_model_pa_s_kernel(tc, attn_ctx, Wo, bo, cluster_probs, out):
                 in_=w_grouped[i][:].rearrange("p s e j -> p (s e j)"),
             )
 
+        def multiply(product, i, s, block, start, stop):
+            nc.tensor.matmul_mx(
+                out=product[:],
+                lhsT=ctx_codes[:, block : block + 2, :].rearrange("p a t -> p (a t)").bitcast(FP8X4),
+                lhsT_scale=ctx_scales[:, block : block + 2, :].rearrange("p a t -> p (a t)"),
+                rhs=w_codes[:, i, s * E : (s + 1) * E].bitcast(FP8X4),
+                rhs_scale=w_scales[:, i, s * E : (s + 1) * E],
+                start=start,
+                stop=stop,
+            )
+
         def multiply_pair(i):
             if not 0 <= i < PAIRS:
                 return
-            products[i] = psum.tile([P, E], F32, name="product%d" % i, tag="bank", bufs=PSUM_BANKS)
-            for s in range(2):
-                tokens = slice(s * TOKENS, s * TOKENS + P)
-                columns = slice(s * E, (s + 1) * E)
-                nc.tensor.matmul_mx(
-                    out=products[i][:],
-                    lhsT=ctx_codes[:, i, tokens].bitcast(FP8X4),
-                    lhsT_scale=ctx_scales[:, i, tokens],
-                    rhs=w_codes[:, i, columns].bitcast(FP8X4),
-                    rhs_scale=w_scales[:, i, columns],
-                    start=(s == 0),
-                    stop=(s == 1),
-                )
+            if i < FOLDED_PAIRS:
+                product = psum.tile([P, E], F32, name="product%d" % i, tag="bank", bufs=PSUM_BANKS)
+                multiply(product, i, 0, 3 * i, True, False)
+                multiply(product, i, 1, 3 * i + 1, False, True)
+                products[i] = [product]
+            else:
+                products[i] = []
+                for s in range(2):
+                    product = psum.tile(
+                        [P, E], F32, name="product%d%d" % (i, s), tag="bank", bufs=PSUM_BANKS
+                    )
+                    multiply(product, i, s, 3 * i + 2 * s, True, True)
+                    products[i].append(product)
+
+        def mix(total, product, rows, c):
+            nc.vector.scalar_tensor_tensor(
+                out=total[rows, :],
+                in0=product[rows, :],
+                scalar=weights[rows, c : c + 1],
+                in1=total[rows, :],
+                op0=MULT,
+                op1=ADD,
+            )
 
         def mix_pair(i):
             if not 0 <= i < PAIRS:
                 return
-            nc.vector.scalar_tensor_tensor(
-                out=mixed[:],
-                in0=products[i][:],
-                scalar=pair_probs[:, i : i + 1],
-                in1=mixed[:],
-                op0=MULT,
-                op1=ADD,
-            )
+            if i < FOLDED_PAIRS:
+                mix(mixed, products[i][0], slice(0, P), 2 * i)
+            else:
+                for s in range(2):
+                    mix(late, products[i][s], slice(0, TOKENS), 2 * i + s)
+            if i == FOLDED_PAIRS - 1:
+                nc.tensor.matmul(
+                    out=fused_psum[:],
+                    lhsT=fold[:].rearrange("p a m -> p (a m)"),
+                    rhs=mixed[:],
+                    start=False,
+                    stop=True,
+                )
 
         transpose_group(0)
         copy_group(0)
@@ -176,9 +202,8 @@ def tile_model_pa_s_kernel(tc, attn_ctx, Wo, bo, cluster_probs, out):
         nc.scalar.copy(out=probs_t[:], in_=probs_t_psum[:])
         fused_psum = psum.tile([P, E], F32, tag="fused")
         nc.tensor.matmul(out=fused_psum[:], lhsT=probs_t[:], rhs=bias_square[:], start=True, stop=False)
-        for s in range(2):
-            rows = slice(s * TOKENS, (s + 1) * TOKENS)
-            nc.vector.tensor_copy(out=pair_probs[rows, :], in_=probs_twice[rows, :, s])
+        nc.vector.tensor_copy(out=weights[0:TOKENS, :], in_=probs_twice[0:TOKENS, :])
+        nc.vector.tensor_copy(out=weights[TOKENS:P, 0 : C - 1], in_=probs_twice[TOKENS:P, 1:C])
 
         for g in range(GROUPS + 2):
             first, second = 2 * g, 2 * g + 1
@@ -194,9 +219,6 @@ def tile_model_pa_s_kernel(tc, attn_ctx, Wo, bo, cluster_probs, out):
             multiply_pair(second - 1)
             mix_pair(second - MIX_LAG)
 
-        nc.tensor.matmul(
-            out=fused_psum[:], lhsT=fold[:].rearrange("p a m -> p (a m)"), rhs=mixed[:], start=False, stop=True
-        )
         fused = keep.tile([TOKENS, E], F32)
-        nc.vector.tensor_copy(out=fused[:], in_=fused_psum[0:TOKENS, :])
+        nc.vector.tensor_add(out=fused[:], in0=fused_psum[0:TOKENS, :], in1=late[:])
         nc.sync.dma_start(out=out.rearrange("b l e -> (b l) e"), in_=fused[:])

@@ -112,12 +112,11 @@ def tile_model_pa_s_kernel(tc, attn_ctx, Wo, bo, cluster_probs, out):
         def quantise_group(g):
             if g >= GROUPS:
                 return
-            for c in range(g * GROUP, (g + 1) * GROUP):
-                i, s = divmod(c, 2)
+            for i in (2 * g, 2 * g + 1):
                 nc.vector.quantize_mx(
-                    out=ctx_codes[:, 3 * i + 2 * s, :].bitcast(FP8X4),
-                    scales=ctx_scales[:, 3 * i + 2 * s, :],
-                    in_=ctx_grouped[:, c, :, :].rearrange("p t j -> p (t j)"),
+                    out=ctx_codes[:, 3 * i + 1 : 3 * i + 3, :].rearrange("p a t -> p (a t)").bitcast(FP8X4),
+                    scales=ctx_scales[:, 3 * i + 1 : 3 * i + 3, :].rearrange("p a t -> p (a t)"),
+                    in_=ctx_grouped[:, 2 * i : 2 * i + 2, :, :].rearrange("p c t j -> p (c t j)"),
                 )
 
         def regroup_pair(i):
@@ -155,7 +154,7 @@ def tile_model_pa_s_kernel(tc, attn_ctx, Wo, bo, cluster_probs, out):
             if i < FOLDED_PAIRS:
                 product = psum.tile([P, E], F32, name="product%d" % i, tag="bank", bufs=PSUM_BANKS)
                 multiply(product, i, 0, 3 * i, True, False)
-                multiply(product, i, 1, 3 * i + 1, False, True)
+                multiply(product, i, 1, 3 * i + 2, False, True)
                 products[i] = [product]
             else:
                 products[i] = []
@@ -163,7 +162,7 @@ def tile_model_pa_s_kernel(tc, attn_ctx, Wo, bo, cluster_probs, out):
                     product = psum.tile(
                         [P, E], F32, name="product%d%d" % (i, s), tag="bank", bufs=PSUM_BANKS
                     )
-                    multiply(product, i, s, 3 * i + 2 * s, True, True)
+                    multiply(product, i, s, 3 * i + 1 + s, True, True)
                     products[i].append(product)
 
         def mix(total, product, rows, c):
@@ -180,7 +179,7 @@ def tile_model_pa_s_kernel(tc, attn_ctx, Wo, bo, cluster_probs, out):
             if not 0 <= i < PAIRS:
                 return
             if i < FOLDED_PAIRS:
-                mix(mixed, products[i][0], slice(0, P), 2 * i)
+                mix(mixed, products[i][0], slice(0, P), 2 * i + 1)
             else:
                 for s in range(2):
                     mix(late, products[i][s], slice(0, TOKENS), 2 * i + s)
@@ -203,7 +202,7 @@ def tile_model_pa_s_kernel(tc, attn_ctx, Wo, bo, cluster_probs, out):
         fused_psum = psum.tile([P, E], F32, tag="fused")
         nc.tensor.matmul(out=fused_psum[:], lhsT=probs_t[:], rhs=bias_square[:], start=True, stop=False)
         nc.vector.tensor_copy(out=weights[0:TOKENS, :], in_=probs_twice[0:TOKENS, :])
-        nc.vector.tensor_copy(out=weights[TOKENS:P, 0 : C - 1], in_=probs_twice[TOKENS:P, 1:C])
+        nc.vector.tensor_copy(out=weights[TOKENS:P, 1:C], in_=probs_twice[TOKENS:P, 0 : C - 1])
 
         for g in range(GROUPS + 2):
             first, second = 2 * g, 2 * g + 1

@@ -38,17 +38,26 @@ def tile_model_pa_s_kernel(tc, attn_ctx, Wo, bo, cluster_probs, out):
     ):
         ctx_raw = []
         w_raw = []
-        for g in range(GROUPS):
+
+        def load_group(g):
             raw = keep.tile([P, B, G], BF16, name="ctx_raw%d" % g)
             nc.sync.dma_start(out=raw[:], in_=ctx_rows[g])
             ctx_raw.append(raw)
-            for i in (2 * g, 2 * g + 1):
-                raw = keep.tile([P, 2, PACK, E], BF16, name="w_raw%d" % i)
-                nc.sync.dma_start(
-                    out=raw[:].rearrange("p s j e -> p s (j e)"),
-                    in_=w_rows[2 * i : 2 * i + 2].rearrange("s (p j) e -> p s (j e)", j=PACK),
-                )
-                w_raw.append(raw)
+
+        def load_pair(i):
+            raw = keep.tile([P, 2, PACK, E], BF16, name="w_raw%d" % i)
+            nc.sync.dma_start(
+                out=raw[:].rearrange("p s j e -> p s (j e)"),
+                in_=w_rows[2 * i : 2 * i + 2].rearrange("s (p j) e -> p s (j e)", j=PACK),
+            )
+            w_raw.append(raw)
+
+        load_group(0)
+        for g in range(GROUPS):
+            load_pair(2 * g)
+            if g + 1 < GROUPS:
+                load_group(g + 1)
+            load_pair(2 * g + 1)
 
         probs_twice = keep.tile([P, C], BF16)
         for s in range(2):
@@ -200,13 +209,14 @@ def tile_model_pa_s_kernel(tc, attn_ctx, Wo, bo, cluster_probs, out):
         probs_t = keep.tile([P, P], BF16)
         nc.scalar.copy(out=probs_t[:], in_=probs_t_psum[:])
         fused_psum = psum.tile([P, E], F32, tag="fused")
-        nc.tensor.matmul(out=fused_psum[:], lhsT=probs_t[:], rhs=bias_square[:], start=True, stop=False)
         nc.vector.tensor_copy(out=weights[0:TOKENS, :], in_=probs_twice[0:TOKENS, :])
         nc.vector.tensor_copy(out=weights[TOKENS:P, 1:C], in_=probs_twice[TOKENS:P, 0 : C - 1])
 
         for g in range(GROUPS + 2):
             first, second = 2 * g, 2 * g + 1
             transpose_group(g + 1)
+            if g == 0:
+                nc.tensor.matmul(out=fused_psum[:], lhsT=probs_t[:], rhs=bias_square[:], start=True, stop=False)
             regroup_pair(first)
             quantise_pair(first - 1)
             quantise_group(g)

@@ -21,6 +21,7 @@ GROUP = P // L
 GROUPS = C // GROUP
 MIX_LAG = 3
 PSUM_BANKS = 6
+VECTOR_COLUMNS = 160
 
 FLOPS = 2 * B * C * L * G * E
 
@@ -46,10 +47,17 @@ def tile_model_pa_s_kernel(tc, attn_ctx, Wo, bo, cluster_probs, out):
 
         def load_pair(i):
             raw = keep.tile([P, 2, PACK, E], BF16, name="w_raw%d" % i)
-            nc.sync.dma_start(
-                out=raw[:].rearrange("p s j e -> p s (j e)"),
-                in_=w_rows[2 * i : 2 * i + 2].rearrange("s (p j) e -> p s (j e)", j=PACK),
-            )
+            if i < PAIRS - 1:
+                nc.sync.dma_start(
+                    out=raw[:].rearrange("p s j e -> p s (j e)"),
+                    in_=w_rows[2 * i : 2 * i + 2].rearrange("s (p j) e -> p s (j e)", j=PACK),
+                )
+            else:
+                for s in range(2):
+                    nc.sync.dma_start(
+                        out=raw[:, s, :, :].rearrange("p j e -> p (j e)"),
+                        in_=w_rows[2 * i + s].rearrange("(p j) e -> p (j e)", j=PACK),
+                    )
             w_raw.append(raw)
 
         load_group(0)
@@ -129,13 +137,27 @@ def tile_model_pa_s_kernel(tc, attn_ctx, Wo, bo, cluster_probs, out):
                 )
 
         def regroup_pair(i):
-            if i >= PAIRS:
-                return
-            for s, copy in ((0, nc.vector.tensor_copy), (1, nc.scalar.copy)):
-                copy(
-                    out=w_grouped[i][:, s, :, :].rearrange("p (g r) j -> p g j r", r=4),
-                    in_=w_raw[i][:, s, :, :].rearrange("p j (g r) -> p g j r", r=4),
-                )
+            vector_columns = VECTOR_COLUMNS if i < PAIRS - 1 else 0
+            for s in range(2):
+                cut = min(max(vector_columns - s * E, 0), E)
+                for copy, cols in ((nc.vector.tensor_copy, slice(0, cut)), (nc.scalar.copy, slice(cut, E))):
+                    if cols.start < cols.stop:
+                        copy(
+                            out=w_grouped[i][:, s, cols, :].rearrange("p (g r) j -> p g j r", r=4),
+                            in_=w_raw[i][:, s, :, cols].rearrange("p j (g r) -> p g j r", r=4),
+                        )
+
+        def quantise_cluster(i, s):
+            nc.vector.quantize_mx(
+                out=w_codes[:, i, s * E : (s + 1) * E].bitcast(FP8X4),
+                scales=w_scales[:, i, s * E : (s + 1) * E],
+                in_=w_grouped[i][:, s, :, :].rearrange("p e j -> p (e j)"),
+            )
+
+        def multiply_cluster(i, s):
+            product = psum.tile([P, E], F32, name="product%d%d" % (i, s), tag="bank", bufs=PSUM_BANKS)
+            multiply(product, i, s, 3 * i + 1 + s, True, True)
+            return product
 
         def quantise_pair(i):
             if not 0 <= i < PAIRS:
@@ -212,7 +234,7 @@ def tile_model_pa_s_kernel(tc, attn_ctx, Wo, bo, cluster_probs, out):
         nc.vector.tensor_copy(out=weights[0:TOKENS, :], in_=probs_twice[0:TOKENS, :])
         nc.vector.tensor_copy(out=weights[TOKENS:P, 1:C], in_=probs_twice[TOKENS:P, 0 : C - 1])
 
-        for g in range(GROUPS + 2):
+        for g in range(GROUPS):
             first, second = 2 * g, 2 * g + 1
             transpose_group(g + 1)
             if g == 0:
@@ -228,6 +250,16 @@ def tile_model_pa_s_kernel(tc, attn_ctx, Wo, bo, cluster_probs, out):
             multiply_pair(second - 1)
             mix_pair(second - MIX_LAG)
 
+        last = PAIRS - 1
+        lower = slice(0, TOKENS)
+        quantise_cluster(last, 0)
+        product_a = multiply_cluster(last, 0)
+        mix_pair(last - 2)
+        quantise_cluster(last, 1)
+        product_b = multiply_cluster(last, 1)
+        mix_pair(last - 1)
+        mix(late, product_a, lower, 2 * last)
+        mix(late, product_b, lower, 2 * last + 1)
         fused = keep.tile([TOKENS, E], F32)
         nc.vector.tensor_add(out=fused[:], in0=fused_psum[0:TOKENS, :], in1=late[:])
         nc.sync.dma_start(out=out.rearrange("b l e -> (b l) e"), in_=fused[:])

@@ -22,6 +22,7 @@ GROUPS = C // GROUP
 MIX_LAG = 3
 PSUM_BANKS = 6
 VECTOR_COLUMNS = 160
+RUN = 8
 
 FLOPS = 2 * B * C * L * G * E
 
@@ -143,8 +144,8 @@ def tile_model_pa_s_kernel(tc, attn_ctx, Wo, bo, cluster_probs, out):
                 for copy, cols in ((nc.vector.tensor_copy, slice(0, cut)), (nc.scalar.copy, slice(cut, E))):
                     if cols.start < cols.stop:
                         copy(
-                            out=w_grouped[i][:, s, cols, :].rearrange("p (g r) j -> p g j r", r=4),
-                            in_=w_raw[i][:, s, :, cols].rearrange("p j (g r) -> p g j r", r=4),
+                            out=w_grouped[i][:, s, cols, :].rearrange("p (g r) j -> p g j r", r=RUN),
+                            in_=w_raw[i][:, s, :, cols].rearrange("p j (g r) -> p g j r", r=RUN),
                         )
 
         def quantise_cluster(i, s):

@@ -21,7 +21,7 @@ GROUP = P // L
 GROUPS = C // GROUP
 MIX_LAG = 3
 PSUM_BANKS = 6
-VECTOR_COLUMNS = 160
+VECTOR_COLUMNS = 144
 RUN = 8
 
 FLOPS = 2 * B * C * L * G * E

@@ -22,6 +22,7 @@ GROUPS = C // GROUP
 MIX_LAG = 3
 PSUM_BANKS = 6
 VECTOR_COLUMNS = 144
+BUSY_PAIRS = (3, 4, 5)
 RUN = 8
 
 FLOPS = 2 * B * C * L * G * E
@@ -188,6 +189,16 @@ def tile_model_pa_s_kernel(tc, attn_ctx, Wo, bo, cluster_probs, out):
                 multiply(product, i, 0, 3 * i, True, False)
                 multiply(product, i, 1, 3 * i + 2, False, True)
                 products[i] = [product]
+                if i in BUSY_PAIRS:
+                    nc.tensor.matmul_mx(
+                        out=busy[:],
+                        lhsT=ctx_codes[:, 3 * i : 3 * i + 2, :].rearrange("p a t -> p (a t)").bitcast(FP8X4),
+                        lhsT_scale=ctx_scales[:, 3 * i : 3 * i + 2, :].rearrange("p a t -> p (a t)"),
+                        rhs=w_codes[:, i - 1 : i + 1, :].rearrange("p i n -> p (i n)").bitcast(FP8X4),
+                        rhs_scale=w_scales[:, i - 1 : i + 1, :].rearrange("p i n -> p (i n)"),
+                        start=True,
+                        stop=True,
+                    )
             else:
                 products[i] = []
                 for s in range(2):
@@ -227,10 +238,11 @@ def tile_model_pa_s_kernel(tc, attn_ctx, Wo, bo, cluster_probs, out):
         transpose_group(0)
         copy_group(0)
 
-        probs_t_psum = psum.tile([P, P], BF16, tag="probs_t")
+        probs_t_psum = psum.tile([P, P], BF16, name="probs_t_psum", tag="spare")
         nc.tensor.transpose(probs_t_psum[:], probs_square[:], ident_bf16[:])
         probs_t = keep.tile([P, P], BF16)
         nc.scalar.copy(out=probs_t[:], in_=probs_t_psum[:])
+        busy = psum.tile([P, 4 * E], F32, name="busy", tag="spare")
         fused_psum = psum.tile([P, E], F32, tag="fused")
         nc.vector.tensor_copy(out=weights[0:TOKENS, :], in_=probs_twice[0:TOKENS, :])
         nc.vector.tensor_copy(out=weights[TOKENS:P, 1:C], in_=probs_twice[TOKENS:P, 0 : C - 1])

import concourse.mybir as mybir
from concourse.masks import make_identity

BF16 = mybir.dt.bfloat16
F32 = mybir.dt.float32
I32 = mybir.dt.int32
U32 = mybir.dt.uint32
U8 = mybir.dt.uint8
FP8X4 = mybir.dt.float8_e4m3fn_x4
MULT = mybir.AluOpType.mult
ADD = mybir.AluOpType.add

P = 128
PACK = 4
B, C, L, G, E = 2, 16, 32, 512, 128
TOKENS = B * L
PAIRS = C // 2
FOLDED_PAIRS = PAIRS - 1
BLOCKS = 3 * PAIRS + 1
GROUP = P // L
GROUPS = C // GROUP
MIX_LAG = 3
PSUM_BANKS = 6
VECTOR_COLUMNS = 144
BUSY_PAIRS = (3, 4, 5)
RUN = 8

FLOPS = 2 * B * C * L * G * E


def tile_model_pa_s_kernel(tc, attn_ctx, Wo, bo, cluster_probs, out):
    nc = tc.nc
    ctx_rows = attn_ctx.rearrange("b (g c) l h d -> g (c l) b (h d)", c=GROUP)
    w_rows = Wo.rearrange("c h d e -> c (h d) e")
    probs_rows = cluster_probs.rearrange("b l c -> (b l) c")

    with (
        tc.tile_pool(name="keep", bufs=1) as keep,
        tc.psum_pool(name="psum", bufs=1) as psum,
        tc.manual_schedule(),
    ):
        ctx_raw = []
        w_raw = []

        def load_group(g):
            raw = keep.tile([P, B, G], BF16, name="ctx_raw%d" % g)
            nc.sync.dma_start(out=raw[:], in_=ctx_rows[g])
            ctx_raw.append(raw)

        def load_pair(i):
            raw = keep.tile([P, 2, PACK, E], BF16, name="w_raw%d" % i)
            if i < PAIRS - 1:
                nc.sync.dma_start(
                    out=raw[:].rearrange("p s j e -> p s (j e)"),
                    in_=w_rows[2 * i : 2 * i + 2].rearrange("s (p j) e -> p s (j e)", j=PACK),
                )
            else:
                for s in range(2):
                    nc.sync.dma_start(
                        out=raw[:, s, :, :].rearrange("p j e -> p (j e)"),
                        in_=w_rows[2 * i + s].rearrange("(p j) e -> p (j e)", j=PACK),
                    )
            w_raw.append(raw)

        load_group(0)
        for g in range(GROUPS):
            load_pair(2 * g)
            if g + 1 < GROUPS:
                load_group(g + 1)
            load_pair(2 * g + 1)

        probs_twice = keep.tile([P, C], BF16)
        for s in range(2):
            nc.scalar.dma_start(out=probs_twice[s * TOKENS : (s + 1) * TOKENS, :], in_=probs_rows)
        probs_square = keep.tile([P, P], BF16)
        nc.vector.memset(probs_square[:], 0.0)
        nc.scalar.dma_start(out=probs_square[0:TOKENS, 0:C], in_=probs_rows)
        bias_square = keep.tile([P, E], BF16)
        nc.vector.memset(bias_square[:], 0.0)
        nc.scalar.dma_start(out=bias_square[0:C, :], in_=bo)

        ident_f32 = keep.tile([P, P], F32)
        make_identity(nc, ident_f32[:])
        ctx_codes = keep.tile([P, BLOCKS, TOKENS], U32, align_bytes=64)
        ctx_scales = keep.tile([P, BLOCKS, TOKENS], U8, align_bytes=64)
        nc.vector.memset(ctx_codes[:].bitcast(I32), 0)
        nc.vector.memset(ctx_scales[:].bitcast(I32), 0)
        mixed = keep.tile([P, E], F32)
        nc.vector.memset(mixed[:], 0.0)
        late = keep.tile([TOKENS, E], F32)
        nc.vector.memset(late[:], 0.0)
        ident_bf16 = keep.tile([P, P], BF16)
        nc.vector.tensor_copy(out=ident_bf16[:], in_=ident_f32[:])
        fold = keep.tile([P, 2, TOKENS], F32)
        for s in range(2):
            nc.vector.tensor_add(
                out=fold[:, s, :], in0=ident_f32[:, 0:TOKENS], in1=ident_f32[:, TOKENS:P]
            )

        ctx_grouped = keep.tile([P, C, TOKENS, PACK], BF16, align_bytes=64)
        ctx_grouped_words = ctx_grouped[:].bitcast(F32)
        ctx_t = {}
        w_codes = keep.tile([P, PAIRS, 2 * E], U32, align_bytes=64)
        w_scales = keep.tile([P, PAIRS, 2 * E], U8, align_bytes=64)
        w_grouped = [
            keep.tile([P, 2, E, PACK], BF16, name="w_grouped%d" % i, align_bytes=64) for i in range(PAIRS)
        ]
        products = {}
        weights = keep.tile([P, C], F32)

        def transpose_group(g):
            if g >= GROUPS:
                return
            words = ctx_raw[g][:].bitcast(F32).rearrange("p b (q u) -> p b u q", u=2)
            for b in range(B):
                ctx_t[(g, b)] = psum.tile(
                    [P, 2, P], F32, name="ctx_t%d%d" % (g, b), tag="bank", bufs=PSUM_BANKS
                )
                for u in range(2):
                    nc.tensor.transpose(ctx_t[(g, b)][:, u, :], words[:, b, u, :], ident_f32[:])

        def copy_group(g):
            if g >= GROUPS:
                return
            for b in range(B):
                nc.scalar.copy(
                    out=ctx_grouped_words[:, g * GROUP : (g + 1) * GROUP, b * L : (b + 1) * L, :],
                    in_=ctx_t[(g, b)][:].rearrange("q u (c l) -> q c l u", l=L),
                )

        def quantise_group(g):
            if g >= GROUPS:
                return
            for i in (2 * g, 2 * g + 1):
                nc.vector.quantize_mx(
                    out=ctx_codes[:, 3 * i + 1 : 3 * i + 3, :].rearrange("p a t -> p (a t)").bitcast(FP8X4),
                    scales=ctx_scales[:, 3 * i + 1 : 3 * i + 3, :].rearrange("p a t -> p (a t)"),
                    in_=ctx_grouped[:, 2 * i : 2 * i + 2, :, :].rearrange("p c t j -> p (c t j)"),
                )

        def regroup_pair(i):
            vector_columns = VECTOR_COLUMNS if i < PAIRS - 1 else 0
            for s in range(2):
                cut = min(max(vector_columns - s * E, 0), E)
                for copy, cols in ((nc.vector.tensor_copy, slice(0, cut)), (nc.scalar.copy, slice(cut, E))):
                    if cols.start < cols.stop:
                        copy(
                            out=w_grouped[i][:, s, cols, :].rearrange("p (g r) j -> p g j r", r=RUN),
                            in_=w_raw[i][:, s, :, cols].rearrange("p j (g r) -> p g j r", r=RUN),
                        )

        def quantise_cluster(i, s):
            nc.vector.quantize_mx(
                out=w_codes[:, i, s * E : (s + 1) * E].bitcast(FP8X4),
                scales=w_scales[:, i, s * E : (s + 1) * E],
                in_=w_grouped[i][:, s, :, :].rearrange("p e j -> p (e j)"),
            )

        def multiply_cluster(i, s):
            product = psum.tile([P, E], F32, name="product%d%d" % (i, s), tag="bank", bufs=PSUM_BANKS)
            multiply(product, i, s, 3 * i + 1 + s, True, True)
            return product

        def quantise_pair(i):
            if not 0 <= i < PAIRS:
                return
            nc.vector.quantize_mx(
                out=w_codes[:, i, :].bitcast(FP8X4),
                scales=w_scales[:, i, :],
                in_=w_grouped[i][:].rearrange("p s e j -> p (s e j)"),
            )

        def multiply(product, i, s, block, start, stop):
            nc.tensor.matmul_mx(
                out=product[:],
                lhsT=ctx_codes[:, block : block + 2, :].rearrange("p a t -> p (a t)").bitcast(FP8X4),
                lhsT_scale=ctx_scales[:, block : block + 2, :].rearrange("p a t -> p (a t)"),
                rhs=w_codes[:, i, s * E : (s + 1) * E].bitcast(FP8X4),
                rhs_scale=w_scales[:, i, s * E : (s + 1) * E],
                start=start,
                stop=stop,
            )

        def multiply_pair(i):
            if not 0 <= i < PAIRS:
                return
            if i < FOLDED_PAIRS:
                product = psum.tile([P, E], F32, name="product%d" % i, tag="bank", bufs=PSUM_BANKS)
                multiply(product, i, 0, 3 * i, True, False)
                multiply(product, i, 1, 3 * i + 2, False, True)
                products[i] = [product]
                if i in BUSY_PAIRS:
                    nc.tensor.matmul_mx(
                        out=busy[:],
                        lhsT=ctx_codes[:, 3 * i : 3 * i + 2, :].rearrange("p a t -> p (a t)").bitcast(FP8X4),
                        lhsT_scale=ctx_scales[:, 3 * i : 3 * i + 2, :].rearrange("p a t -> p (a t)"),
                        rhs=w_codes[:, i - 1 : i + 1, :].rearrange("p i n -> p (i n)").bitcast(FP8X4),
                        rhs_scale=w_scales[:, i - 1 : i + 1, :].rearrange("p i n -> p (i n)"),
                        start=True,
                        stop=True,
                    )
            else:
                products[i] = []
                for s in range(2):
                    product = psum.tile(
                        [P, E], F32, name="product%d%d" % (i, s), tag="bank", bufs=PSUM_BANKS
                    )
                    multiply(product, i, s, 3 * i + 1 + s, True, True)
                    products[i].append(product)

        def mix(total, product, rows, c):
            nc.vector.scalar_tensor_tensor(
                out=total[rows, :],
                in0=product[rows, :],
                scalar=weights[rows, c : c + 1],
                in1=total[rows, :],
                op0=MULT,
                op1=ADD,
            )

        def mix_pair(i):
            if not 0 <= i < PAIRS:
                return
            if i < FOLDED_PAIRS:
                mix(mixed, products[i][0], slice(0, P), 2 * i + 1)
            else:
                for s in range(2):
                    mix(late, products[i][s], slice(0, TOKENS), 2 * i + s)
            if i == FOLDED_PAIRS - 1:
                nc.tensor.matmul(
                    out=fused_psum[:],
                    lhsT=fold[:].rearrange("p a m -> p (a m)"),
                    rhs=mixed[:],
                    start=False,
                    stop=True,
                )

        transpose_group(0)
        copy_group(0)

        probs_t_psum = psum.tile([P, P], BF16, name="probs_t_psum", tag="spare")
        nc.tensor.transpose(probs_t_psum[:], probs_square[:], ident_bf16[:])
        probs_t = keep.tile([P, P], BF16)
        nc.scalar.copy(out=probs_t[:], in_=probs_t_psum[:])
        busy = psum.tile([P, 4 * E], F32, name="busy", tag="spare")
        fused_psum = psum.tile([P, E], F32, tag="fused")
        nc.vector.tensor_copy(out=weights[0:TOKENS, :], in_=probs_twice[0:TOKENS, :])
        nc.vector.tensor_copy(out=weights[TOKENS:P, 1:C], in_=probs_twice[TOKENS:P, 0 : C - 1])

        for g in range(GROUPS):
            first, second = 2 * g, 2 * g + 1
            transpose_group(g + 1)
            if g == 0:
                nc.tensor.matmul(out=fused_psum[:], lhsT=probs_t[:], rhs=bias_square[:], start=True, stop=False)
            regroup_pair(first)
            quantise_pair(first - 1)
            quantise_group(g)
            multiply_pair(first - 1)
            mix_pair(first - MIX_LAG)
            regroup_pair(second)
            copy_group(g + 1)
            quantise_pair(second - 1)
            multiply_pair(second - 1)
            mix_pair(second - MIX_LAG)

        last = PAIRS - 1
        lower = slice(0, TOKENS)
        quantise_cluster(last, 0)
        product_a = multiply_cluster(last, 0)
        mix_pair(last - 2)
        quantise_cluster(last, 1)
        product_b = multiply_cluster(last, 1)
        mix_pair(last - 1)
        mix(late, product_a, lower, 2 * last)
        mix(late, product_b, lower, 2 * last + 1)
        fused = keep.tile([TOKENS, E], F32)
        nc.vector.tensor_add(out=fused[:], in0=fused_psum[0:TOKENS, :], in1=late[:])
        nc.sync.dma_start(out=out.rearrange("b l e -> (b l) e"), in_=fused[:])
